import numpy as np
import ml_dtypes

BF16 = ml_dtypes.bfloat16


def bf(x):
    return np.asarray(x, np.float32).astype(BF16)


def f32(x):
    return np.asarray(x, np.float32)


def f64(x):
    return np.asarray(x).astype(np.float64)


def striped(idx):
    return np.tile(idx.reshape(-1, 16).T, (8, 1))


C, S, M, T, R, H, K, N = 256, 512, 128, 3, 16, 256, 6, 1536
KEEP = 0.75


def setup_inputs():
    x = f32(np.random.standard_normal((C, S)))
    w = f32(0.5 * np.random.standard_normal((R, S, M)))
    mask = f32(np.random.random((S, M)) < KEEP)
    gamma = f32(-0.25 + 0.02 * np.random.standard_normal((1,)))
    idx = np.concatenate([np.random.permutation(S)[:H] for _ in range(K)])
    return {"x": x, "w": w, "mask": mask, "gamma": gamma, "offs": striped(idx)}


def reference(x, w, mask, gamma, offs):
    idx = offs[:16].T.reshape(-1)
    x = f64(x)
    u = x[:, idx].reshape(C, T, S)
    streams = [x] + [u[:, t] for t in range(T)]
    pos = [np.maximum(s, 0.0) for s in streams]
    neg = [np.maximum(-s, 0.0) for s in streams]
    f = np.empty((C, R, S))
    for r in range(R):
        v = np.ones((C, S))
        for t in range(T + 1):
            v = v * (neg[t] if (r >> (T - t)) & 1 else pos[t])
        f[:, r] = v
    wb = np.sign(f64(w)) * f64(mask)[None]
    return np.abs(f64(gamma)[0]) * (f.reshape(C, R * S) @ wb.reshape(R * S, M))

@@ -1,0 +1,127 @@
+import concourse.mybir as mybir
+from concourse.masks import make_identity
+
+F32 = mybir.dt.float32
+BF16 = mybir.dt.bfloat16
+U16 = mybir.dt.uint16
+ALU = mybir.AluOpType
+FUNC = mybir.ActivationFunctionType
+
+P = 128
+C, S, M, R, T = 256, 512, 128, 16, 3
+CB = C // P
+J = S // P
+HALF = 2
+COLS = S // 16
+ROWS = 2
+
+FLOPS = 2 * C * R * S * M
+
+
+def every_jth(tile):
+    return tile[:].rearrange("c (p j) -> c j p", j=J)
+
+
+def tile_binary_dense_kernel(tc, x, w, mask, gamma, offs, out):
+    nc = tc.nc
+    with (
+        tc.tile_pool(name="held", bufs=1) as held,
+        tc.psum_pool(name="psum", bufs=1) as psum,
+    ):
+        offsets = held.tile([P, T * COLS], U16, name="offsets")
+        nc.sync.dma_start(offsets[:], offs)
+        window = [held.tile([P, S], F32, name=f"window{cb}") for cb in range(CB)]
+        chain = [[held.tile([P, S], F32, name=f"chain{t}_{cb}") for cb in range(CB)] for t in range(T + 1)]
+        for cb in range(CB):
+            samples = x[cb * P : (cb + 1) * P, :]
+            nc.sync.dma_start(window[cb][:], samples)
+            nc.sync.dma_start(chain[0][cb][:], samples)
+
+        mask_f32 = held.tile([P, J * M], F32, name="mask_f32")
+        nc.gpsimd.dma_start(mask_f32[:], mask.rearrange("(p j) m -> p (j m)", j=J))
+        gamma_all = held.tile([P, 1], F32, name="gamma_all")
+        nc.gpsimd.dma_start(gamma_all[:], gamma.partition_broadcast(P))
+
+        w_by_partition = w.rearrange("r (p j) m -> p r (j m)", j=J)
+        w_raw = [held.tile([P, ROWS, J * M], F32, name=f"w_raw{g}") for g in range(R // ROWS)]
+        for g in range(R // ROWS):
+            nc.sync.dma_start(w_raw[g][:], w_by_partition[:, g * ROWS : (g + 1) * ROWS, :])
+
+        eye = held.tile([P, P], F32, name="eye")
+        make_identity(nc, eye[:])
+        weighted_eye = [held.tile([P, P], BF16, name=f"weighted_eye{t}") for t in range(T)]
+        for t in range(T):
+            nc.vector.tensor_scalar_mul(weighted_eye[t][:], eye[:], float(2 ** (T - 1 - t)))
+        mask_bf16 = held.tile([P, J * M], BF16, name="mask_bf16")
+        nc.vector.tensor_copy(mask_bf16[:], mask_f32[:])
+        abs_gamma = held.tile([P, 1], F32, name="abs_gamma")
+        nc.scalar.activation(abs_gamma[:], gamma_all[:], FUNC.Abs)
+
+        sign_of = [[held.tile([P, S], BF16, name=f"sign_of{t}_{cb}") for cb in range(CB)] for t in range(T)]
+        for t in range(T):
+            for cb in range(CB):
+                nc.scalar.activation(sign_of[t][cb][:], chain[t][cb][:], FUNC.Sign)
+                looked_up = window[cb][:].indirect(offsets[:, t * COLS : (t + 1) * COLS])
+                nc.vector.tensor_tensor(chain[t + 1][cb][:], looked_up, chain[t][cb][:], ALU.mult)
+
+        signs_turned = held.tile([P, J, C], BF16, name="signs_turned")
+        for h in range(J // HALF):
+            signs_bank = psum.tile([P, HALF, C], F32, name=f"signs_bank{h}")
+            for k in range(HALF):
+                for cb in range(CB):
+                    for t in range(T):
+                        nc.tensor.matmul(
+                            signs_bank[:, k, cb * P : (cb + 1) * P],
+                            lhsT=every_jth(sign_of[t][cb])[:, h * HALF + k, :],
+                            rhs=weighted_eye[t][:],
+                            start=(t == 0),
+                            stop=(t == T - 1),
+                        )
+            nc.scalar.copy(signs_turned[:, h * HALF : (h + 1) * HALF, :], signs_bank[:])
+
+        magnitude = [held.tile([P, J, C], BF16, name=f"magnitude{n3}") for n3 in range(2)]
+        for h in range(J // HALF):
+            last_bank = psum.tile([P, HALF, C], F32, name=f"last_bank{h}")
+            for k in range(HALF):
+                for cb in range(CB):
+                    nc.tensor.transpose(
+                        last_bank[:, k, cb * P : (cb + 1) * P],
+                        every_jth(chain[T][cb])[:, h * HALF + k, :],
+                        eye[:],
+                    )
+            for n3 in range(2):
+                nc.scalar.activation(
+                    magnitude[n3][:, h * HALF : (h + 1) * HALF, :], last_bank[:], FUNC.Relu, scale=1.0 - 2.0 * n3
+                )
+
+        matches = [held.tile([P, J, C], BF16, name=f"matches{n}") for n in range(R // 2)]
+        for n in range(R // 2):
+            nc.vector.tensor_scalar(matches[n][:], signs_turned[:], float(R // 2 - 1 - 2 * n), None, ALU.is_equal)
+
+        weights = [held.tile([P, ROWS, J * M], BF16, name=f"weights{g}") for g in range(R // ROWS)]
+        for g in range(R // ROWS):
+            w_sign = held.tile([P, ROWS, J * M], BF16, name=f"w_sign{g}")
+            nc.scalar.activation(w_sign[:], w_raw[g][:], FUNC.Sign)
+            nc.vector.tensor_tensor(
+                weights[g][:], w_sign[:], mask_bf16[:].unsqueeze(1).to_broadcast([P, ROWS, J * M]), ALU.mult
+            )
+
+        acc = [psum.tile([P, M], F32, name=f"acc{cb}") for cb in range(CB)]
+        for r in range(R):
+            code = r ^ (r >> 1) ^ (r >> 2) ^ (r >> 3)
+            f_row = held.tile([P, J, C], BF16, name=f"f_row{r}")
+            nc.vector.tensor_tensor(f_row[:], magnitude[code & 1][:], matches[code >> 1][:], ALU.mult)
+            for j in range(J):
+                for cb in range(CB):
+                    nc.tensor.matmul(
+                        acc[cb][:],
+                        lhsT=f_row[:, j, cb * P : (cb + 1) * P],
+                        rhs=weights[r // ROWS][:, r % ROWS, j * M : (j + 1) * M],
+                        start=(r == 0 and j == 0),
+                        stop=(r == R - 1 and j == J - 1),
+                    )
+
+        for cb in range(CB):
+            scaled = held.tile([P, M], F32, name=f"scaled{cb}")
+            nc.vector.tensor_scalar_mul(scaled[:], acc[cb][:], abs_gamma[:, 0:1])
+            nc.sync.dma_start(out[cb * P : (cb + 1) * P, :], scaled[:])

@@ -13,7 +13,7 @@ CB = C // P
 J = S // P
 HALF = 2
 COLS = S // 16
-ROWS = 2
+EARLY = (T - 1) * CB
 
 FLOPS = 2 * C * R * S * M
 
@@ -36,75 +36,71 @@ def tile_binary_dense_kernel(tc, x, w, mask, gamma, offs, out):
             samples = x[cb * P : (cb + 1) * P, :]
             nc.sync.dma_start(window[cb][:], samples)
             nc.sync.dma_start(chain[0][cb][:], samples)
-
         mask_f32 = held.tile([P, J * M], F32, name="mask_f32")
-        nc.gpsimd.dma_start(mask_f32[:], mask.rearrange("(p j) m -> p (j m)", j=J))
-        gamma_all = held.tile([P, 1], F32, name="gamma_all")
-        nc.gpsimd.dma_start(gamma_all[:], gamma.partition_broadcast(P))
-
+        nc.sync.dma_start(mask_f32[:], mask.rearrange("(p j) m -> p (j m)", j=J))
         w_by_partition = w.rearrange("r (p j) m -> p r (j m)", j=J)
-        w_raw = [held.tile([P, ROWS, J * M], F32, name=f"w_raw{g}") for g in range(R // ROWS)]
-        for g in range(R // ROWS):
-            nc.sync.dma_start(w_raw[g][:], w_by_partition[:, g * ROWS : (g + 1) * ROWS, :])
+        w_raw = [held.tile([P, J * M], F32, name=f"w_raw{r}") for r in range(R)]
+        for r in range(R):
+            nc.sync.dma_start(w_raw[r][:], w_by_partition[:, r, :])
+        gamma_all = held.tile([P, 1], F32, name="gamma_all")
+        nc.sync.dma_start(gamma_all[:], gamma.partition_broadcast(P))
 
         eye = held.tile([P, P], F32, name="eye")
         make_identity(nc, eye[:])
         weighted_eye = [held.tile([P, P], BF16, name=f"weighted_eye{t}") for t in range(T)]
         for t in range(T):
-            nc.vector.tensor_scalar_mul(weighted_eye[t][:], eye[:], float(2 ** (T - 1 - t)))
+            nc.scalar.mul(weighted_eye[t][:], eye[:], float(2 ** (T - 1 - t)))
+
+        weights = [held.tile([P, J * M], BF16, name=f"weights{r}") for r in range(R)]
         mask_bf16 = held.tile([P, J * M], BF16, name="mask_bf16")
-        nc.vector.tensor_copy(mask_bf16[:], mask_f32[:])
-        abs_gamma = held.tile([P, 1], F32, name="abs_gamma")
-        nc.scalar.activation(abs_gamma[:], gamma_all[:], FUNC.Abs)
+        nc.gpsimd.tensor_copy(mask_bf16[:], mask_f32[:])
+        w_sign = [held.tile([P, J * M], BF16, name=f"w_sign{r}") for r in range(EARLY)]
+        w_masked = [held.tile([P, J * M], F32, name=f"w_masked{r}") for r in range(EARLY, R)]
+        for r in range(EARLY, R):
+            nc.gpsimd.tensor_tensor(w_masked[r - EARLY][:], w_raw[r][:], mask_f32[:], ALU.mult)
 
         sign_of = [[held.tile([P, S], BF16, name=f"sign_of{t}_{cb}") for cb in range(CB)] for t in range(T)]
+        signs_bank = [psum.tile([P, HALF, C], F32, name=f"signs_bank{h}") for h in range(J // HALF)]
         for t in range(T):
             for cb in range(CB):
-                nc.scalar.activation(sign_of[t][cb][:], chain[t][cb][:], FUNC.Sign)
                 looked_up = window[cb][:].indirect(offsets[:, t * COLS : (t + 1) * COLS])
                 nc.vector.tensor_tensor(chain[t + 1][cb][:], looked_up, chain[t][cb][:], ALU.mult)
-
+                nc.scalar.activation(sign_of[t][cb][:], chain[t][cb][:], FUNC.Sign)
+                if t > 0:
+                    early_row = (t - 1) * CB + cb
+                    nc.scalar.activation(w_sign[early_row][:], w_raw[early_row][:], FUNC.Sign)
+                for j in range(J):
+                    nc.tensor.matmul(
+                        signs_bank[j // HALF][:, j % HALF, cb * P : (cb + 1) * P],
+                        lhsT=every_jth(sign_of[t][cb])[:, j, :],
+                        rhs=weighted_eye[t][:],
+                        start=(t == 0 and cb == 0 and j % HALF == 0),
+                        stop=(t == T - 1 and cb == CB - 1 and j % HALF == HALF - 1),
+                    )
+        for r in range(EARLY):
+            nc.vector.tensor_tensor(weights[r][:], w_sign[r][:], mask_bf16[:], ALU.mult)
         signs_turned = held.tile([P, J, C], BF16, name="signs_turned")
         for h in range(J // HALF):
-            signs_bank = psum.tile([P, HALF, C], F32, name=f"signs_bank{h}")
-            for k in range(HALF):
-                for cb in range(CB):
-                    for t in range(T):
-                        nc.tensor.matmul(
-                            signs_bank[:, k, cb * P : (cb + 1) * P],
-                            lhsT=every_jth(sign_of[t][cb])[:, h * HALF + k, :],
-                            rhs=weighted_eye[t][:],
-                            start=(t == 0),
-                            stop=(t == T - 1),
-                        )
-            nc.scalar.copy(signs_turned[:, h * HALF : (h + 1) * HALF, :], signs_bank[:])
-
-        magnitude = [held.tile([P, J, C], BF16, name=f"magnitude{n3}") for n3 in range(2)]
-        for h in range(J // HALF):
-            last_bank = psum.tile([P, HALF, C], F32, name=f"last_bank{h}")
-            for k in range(HALF):
-                for cb in range(CB):
-                    nc.tensor.transpose(
-                        last_bank[:, k, cb * P : (cb + 1) * P],
-                        every_jth(chain[T][cb])[:, h * HALF + k, :],
-                        eye[:],
-                    )
-            for n3 in range(2):
-                nc.scalar.activation(
-                    magnitude[n3][:, h * HALF : (h + 1) * HALF, :], last_bank[:], FUNC.Relu, scale=1.0 - 2.0 * n3
-                )
+            nc.scalar.copy(signs_turned[:, h * HALF : (h + 1) * HALF, :], signs_bank[h][:])
 
         matches = [held.tile([P, J, C], BF16, name=f"matches{n}") for n in range(R // 2)]
         for n in range(R // 2):
             nc.vector.tensor_scalar(matches[n][:], signs_turned[:], float(R // 2 - 1 - 2 * n), None, ALU.is_equal)
 
-        weights = [held.tile([P, ROWS, J * M], BF16, name=f"weights{g}") for g in range(R // ROWS)]
-        for g in range(R // ROWS):
-            w_sign = held.tile([P, ROWS, J * M], BF16, name=f"w_sign{g}")
-            nc.scalar.activation(w_sign[:], w_raw[g][:], FUNC.Sign)
-            nc.vector.tensor_tensor(
-                weights[g][:], w_sign[:], mask_bf16[:].unsqueeze(1).to_broadcast([P, ROWS, J * M]), ALU.mult
-            )
+        magnitude = [held.tile([P, J, C], BF16, name=f"magnitude{n3}") for n3 in range(2)]
+        last_bank = [psum.tile([P, HALF, C], F32, name=f"last_bank{h}") for h in range(J // HALF)]
+        for cb in range(CB):
+            for j in range(J):
+                nc.tensor.transpose(
+                    last_bank[j // HALF][:, j % HALF, cb * P : (cb + 1) * P], every_jth(chain[T][cb])[:, j, :], eye[:]
+                )
+        for n3 in range(2):
+            for h in range(J // HALF):
+                nc.scalar.activation(
+                    magnitude[n3][:, h * HALF : (h + 1) * HALF, :], last_bank[h][:], FUNC.Relu, scale=1.0 - 2.0 * n3
+                )
+        for r in range(EARLY, R):
+            nc.scalar.activation(weights[r][:], w_masked[r - EARLY][:], FUNC.Sign)
 
         acc = [psum.tile([P, M], F32, name=f"acc{cb}") for cb in range(CB)]
         for r in range(R):
@@ -116,11 +112,13 @@ def tile_binary_dense_kernel(tc, x, w, mask, gamma, offs, out):
                     nc.tensor.matmul(
                         acc[cb][:],
                         lhsT=f_row[:, j, cb * P : (cb + 1) * P],
-                        rhs=weights[r // ROWS][:, r % ROWS, j * M : (j + 1) * M],
+                        rhs=weights[r][:, j * M : (j + 1) * M],
                         start=(r == 0 and j == 0),
                         stop=(r == R - 1 and j == J - 1),
                     )
 
+        abs_gamma = held.tile([P, 1], F32, name="abs_gamma")
+        nc.scalar.activation(abs_gamma[:], gamma_all[:], FUNC.Abs)
         for cb in range(CB):
             scaled = held.tile([P, M], F32, name=f"scaled{cb}")
             nc.vector.tensor_scalar_mul(scaled[:], acc[cb][:], abs_gamma[:, 0:1])

@@ -11,7 +11,6 @@ P = 128
 C, S, M, R, T = 256, 512, 128, 16, 3
 CB = C // P
 J = S // P
-HALF = 2
 COLS = S // 16
 EARLY = (T - 1) * CB
 
@@ -47,71 +46,68 @@ def tile_binary_dense_kernel(tc, x, w, mask, gamma, offs, out):
 
         eye = held.tile([P, P], F32, name="eye")
         make_identity(nc, eye[:])
+        mask_bf16 = held.tile([P, J * M], BF16, name="mask_bf16")
+        nc.gpsimd.tensor_copy(mask_bf16[:], mask_f32[:])
         weighted_eye = [held.tile([P, P], BF16, name=f"weighted_eye{t}") for t in range(T)]
         for t in range(T):
             nc.scalar.mul(weighted_eye[t][:], eye[:], float(2 ** (T - 1 - t)))
 
+        w_sign = [held.tile([P, J * M], BF16, name=f"w_sign{r}") for r in range(R)]
         weights = [held.tile([P, J * M], BF16, name=f"weights{r}") for r in range(R)]
-        mask_bf16 = held.tile([P, J * M], BF16, name="mask_bf16")
-        nc.gpsimd.tensor_copy(mask_bf16[:], mask_f32[:])
-        w_sign = [held.tile([P, J * M], BF16, name=f"w_sign{r}") for r in range(EARLY)]
-        w_masked = [held.tile([P, J * M], F32, name=f"w_masked{r}") for r in range(EARLY, R)]
-        for r in range(EARLY, R):
-            nc.gpsimd.tensor_tensor(w_masked[r - EARLY][:], w_raw[r][:], mask_f32[:], ALU.mult)
+
+        def take_sign(r):
+            nc.scalar.activation(w_sign[r][:], w_raw[r][:], FUNC.Sign)
+
+        def apply_mask(r):
+            nc.vector.tensor_tensor(weights[r][:], w_sign[r][:], mask_bf16[:], ALU.mult)
 
         sign_of = [[held.tile([P, S], BF16, name=f"sign_of{t}_{cb}") for cb in range(CB)] for t in range(T)]
-        signs_bank = [psum.tile([P, HALF, C], F32, name=f"signs_bank{h}") for h in range(J // HALF)]
         for t in range(T):
             for cb in range(CB):
                 looked_up = window[cb][:].indirect(offsets[:, t * COLS : (t + 1) * COLS])
                 nc.vector.tensor_tensor(chain[t + 1][cb][:], looked_up, chain[t][cb][:], ALU.mult)
                 nc.scalar.activation(sign_of[t][cb][:], chain[t][cb][:], FUNC.Sign)
                 if t > 0:
-                    early_row = (t - 1) * CB + cb
-                    nc.scalar.activation(w_sign[early_row][:], w_raw[early_row][:], FUNC.Sign)
-                for j in range(J):
+                    take_sign((t - 1) * CB + cb)
+
+        signs_turned = held.tile([P, CB, J, P], BF16, name="signs_turned")
+        magnitude = [held.tile([P, CB, J, P], BF16, name=f"magnitude{n3}") for n3 in range(2)]
+        matches = [held.tile([P, CB, J, P], BF16, name=f"matches{n}") for n in range(R // 2)]
+        for cb in range(CB):
+            signs_bank = psum.tile([P, J, P], F32, name=f"signs_bank{cb}")
+            for j in range(J):
+                for t in range(T):
                     nc.tensor.matmul(
-                        signs_bank[j // HALF][:, j % HALF, cb * P : (cb + 1) * P],
+                        signs_bank[:, j, :],
                         lhsT=every_jth(sign_of[t][cb])[:, j, :],
                         rhs=weighted_eye[t][:],
-                        start=(t == 0 and cb == 0 and j % HALF == 0),
-                        stop=(t == T - 1 and cb == CB - 1 and j % HALF == HALF - 1),
+                        start=(t == 0),
+                        stop=(t == T - 1),
                     )
-        for r in range(EARLY):
-            nc.vector.tensor_tensor(weights[r][:], w_sign[r][:], mask_bf16[:], ALU.mult)
-        signs_turned = held.tile([P, J, C], BF16, name="signs_turned")
-        for h in range(J // HALF):
-            nc.scalar.copy(signs_turned[:, h * HALF : (h + 1) * HALF, :], signs_bank[h][:])
-
-        matches = [held.tile([P, J, C], BF16, name=f"matches{n}") for n in range(R // 2)]
-        for n in range(R // 2):
-            nc.vector.tensor_scalar(matches[n][:], signs_turned[:], float(R // 2 - 1 - 2 * n), None, ALU.is_equal)
-
-        magnitude = [held.tile([P, J, C], BF16, name=f"magnitude{n3}") for n3 in range(2)]
-        last_bank = [psum.tile([P, HALF, C], F32, name=f"last_bank{h}") for h in range(J // HALF)]
-        for cb in range(CB):
+            nc.scalar.copy(signs_turned[:, cb], signs_bank[:])
+            last_bank = psum.tile([P, J, P], F32, name=f"last_bank{cb}")
             for j in range(J):
-                nc.tensor.transpose(
-                    last_bank[j // HALF][:, j % HALF, cb * P : (cb + 1) * P], every_jth(chain[T][cb])[:, j, :], eye[:]
-                )
-        for n3 in range(2):
-            for h in range(J // HALF):
-                nc.scalar.activation(
-                    magnitude[n3][:, h * HALF : (h + 1) * HALF, :], last_bank[h][:], FUNC.Relu, scale=1.0 - 2.0 * n3
+                nc.tensor.transpose(last_bank[:, j, :], every_jth(chain[T][cb])[:, j, :], eye[:])
+            for n3 in range(2):
+                nc.scalar.activation(magnitude[n3][:, cb], last_bank[:], FUNC.Relu, scale=1.0 - 2.0 * n3)
+            for n in range(R // 2):
+                nc.vector.tensor_scalar(
+                    matches[n][:, cb], signs_turned[:, cb], float(R // 2 - 1 - 2 * n), None, ALU.is_equal
                 )
         for r in range(EARLY, R):
-            nc.scalar.activation(weights[r][:], w_masked[r - EARLY][:], FUNC.Sign)
+            take_sign(r)
 
         acc = [psum.tile([P, M], F32, name=f"acc{cb}") for cb in range(CB)]
         for r in range(R):
             code = r ^ (r >> 1) ^ (r >> 2) ^ (r >> 3)
-            f_row = held.tile([P, J, C], BF16, name=f"f_row{r}")
+            apply_mask(r)
+            f_row = held.tile([P, CB, J, P], BF16, name=f"f_row{r}")
             nc.vector.tensor_tensor(f_row[:], magnitude[code & 1][:], matches[code >> 1][:], ALU.mult)
             for j in range(J):
                 for cb in range(CB):
                     nc.tensor.matmul(
                         acc[cb][:],
-                        lhsT=f_row[:, j, cb * P : (cb + 1) * P],
+                        lhsT=f_row[:, cb, j, :],
                         rhs=weights[r][:, j * M : (j + 1) * M],
                         start=(r == 0 and j == 0),
                         stop=(r == R - 1 and j == J - 1),

@@ -12,7 +12,9 @@ C, S, M, R, T = 256, 512, 128, 16, 3
 CB = C // P
 J = S // P
 COLS = S // 16
-EARLY = (T - 1) * CB
+PAIR = 2
+PAIRS = R // PAIR
+AHEAD = 2
 
 FLOPS = 2 * C * R * S * M
 
@@ -38,9 +40,9 @@ def tile_binary_dense_kernel(tc, x, w, mask, gamma, offs, out):
         mask_f32 = held.tile([P, J * M], F32, name="mask_f32")
         nc.sync.dma_start(mask_f32[:], mask.rearrange("(p j) m -> p (j m)", j=J))
         w_by_partition = w.rearrange("r (p j) m -> p r (j m)", j=J)
-        w_raw = [held.tile([P, J * M], F32, name=f"w_raw{r}") for r in range(R)]
+        w_raw = held.tile([P, R, J * M], F32, name="w_raw")
         for r in range(R):
-            nc.sync.dma_start(w_raw[r][:], w_by_partition[:, r, :])
+            nc.sync.dma_start(w_raw[:, r, :], w_by_partition[:, r, :])
         gamma_all = held.tile([P, 1], F32, name="gamma_all")
         nc.sync.dma_start(gamma_all[:], gamma.partition_broadcast(P))
 
@@ -52,14 +54,16 @@ def tile_binary_dense_kernel(tc, x, w, mask, gamma, offs, out):
         for t in range(T):
             nc.scalar.mul(weighted_eye[t][:], eye[:], float(2 ** (T - 1 - t)))
 
-        w_sign = [held.tile([P, J * M], BF16, name=f"w_sign{r}") for r in range(R)]
-        weights = [held.tile([P, J * M], BF16, name=f"weights{r}") for r in range(R)]
+        w_sign = [held.tile([P, PAIR, J * M], BF16, name=f"w_sign{g}") for g in range(PAIRS)]
+        weights = [held.tile([P, PAIR, J * M], BF16, name=f"weights{g}") for g in range(PAIRS)]
 
         def take_sign(r):
-            nc.scalar.activation(w_sign[r][:], w_raw[r][:], FUNC.Sign)
+            nc.scalar.activation(w_sign[r // PAIR][:, r % PAIR, :], w_raw[:, r, :], FUNC.Sign)
 
-        def apply_mask(r):
-            nc.vector.tensor_tensor(weights[r][:], w_sign[r][:], mask_bf16[:], ALU.mult)
+        def apply_mask(g):
+            nc.vector.tensor_tensor(
+                weights[g][:], w_sign[g][:], mask_bf16[:].unsqueeze(1).to_broadcast([P, PAIR, J * M]), ALU.mult
+            )
 
         sign_of = [[held.tile([P, S], BF16, name=f"sign_of{t}_{cb}") for cb in range(CB)] for t in range(T)]
         for t in range(T):
@@ -69,38 +73,48 @@ def tile_binary_dense_kernel(tc, x, w, mask, gamma, offs, out):
                 nc.scalar.activation(sign_of[t][cb][:], chain[t][cb][:], FUNC.Sign)
                 if t > 0:
                     take_sign((t - 1) * CB + cb)
+        for g in range(AHEAD):
+            apply_mask(g)
 
+        plain_eye = weighted_eye[T - 1]
+        magnitude_rows = [[held.tile([P, S], BF16, name=f"magnitude_rows{n3}_{cb}") for cb in range(CB)] for n3 in range(2)]
+        magnitude = [psum.tile([P, CB, J, P], BF16, name=f"magnitude{n3}") for n3 in range(2)]
+        signs_bank = [psum.tile([P, J, P], F32, name=f"signs_bank{cb}") for cb in range(CB)]
         signs_turned = held.tile([P, CB, J, P], BF16, name="signs_turned")
-        magnitude = [held.tile([P, CB, J, P], BF16, name=f"magnitude{n3}") for n3 in range(2)]
         matches = [held.tile([P, CB, J, P], BF16, name=f"matches{n}") for n in range(R // 2)]
         for cb in range(CB):
-            signs_bank = psum.tile([P, J, P], F32, name=f"signs_bank{cb}")
             for j in range(J):
                 for t in range(T):
                     nc.tensor.matmul(
-                        signs_bank[:, j, :],
+                        signs_bank[cb][:, j, :],
                         lhsT=every_jth(sign_of[t][cb])[:, j, :],
                         rhs=weighted_eye[t][:],
                         start=(t == 0),
                         stop=(t == T - 1),
                     )
-            nc.scalar.copy(signs_turned[:, cb], signs_bank[:])
-            last_bank = psum.tile([P, J, P], F32, name=f"last_bank{cb}")
-            for j in range(J):
-                nc.tensor.transpose(last_bank[:, j, :], every_jth(chain[T][cb])[:, j, :], eye[:])
+        for cb in range(CB):
             for n3 in range(2):
-                nc.scalar.activation(magnitude[n3][:, cb], last_bank[:], FUNC.Relu, scale=1.0 - 2.0 * n3)
+                nc.scalar.activation(magnitude_rows[n3][cb][:], chain[T][cb][:], FUNC.Relu, scale=1.0 - 2.0 * n3)
+            nc.scalar.copy(signs_turned[:, cb], signs_bank[cb][:])
+            for n3 in range(2):
+                for j in range(J):
+                    nc.tensor.matmul(
+                        magnitude[n3][:, cb, j, :],
+                        lhsT=every_jth(magnitude_rows[n3][cb])[:, j, :],
+                        rhs=plain_eye[:],
+                        start=True,
+                        stop=True,
+                    )
             for n in range(R // 2):
                 nc.vector.tensor_scalar(
                     matches[n][:, cb], signs_turned[:, cb], float(R // 2 - 1 - 2 * n), None, ALU.is_equal
                 )
-        for r in range(EARLY, R):
+        for r in range(AHEAD * PAIR, R):
             take_sign(r)
 
         acc = [psum.tile([P, M], F32, name=f"acc{cb}") for cb in range(CB)]
         for r in range(R):
             code = r ^ (r >> 1) ^ (r >> 2) ^ (r >> 3)
-            apply_mask(r)
             f_row = held.tile([P, CB, J, P], BF16, name=f"f_row{r}")
             nc.vector.tensor_tensor(f_row[:], magnitude[code & 1][:], matches[code >> 1][:], ALU.mult)
             for j in range(J):
@@ -108,10 +122,12 @@ def tile_binary_dense_kernel(tc, x, w, mask, gamma, offs, out):
                     nc.tensor.matmul(
                         acc[cb][:],
                         lhsT=f_row[:, cb, j, :],
-                        rhs=weights[r][:, j * M : (j + 1) * M],
+                        rhs=weights[r // PAIR][:, r % PAIR, j * M : (j + 1) * M],
                         start=(r == 0 and j == 0),
                         stop=(r == R - 1 and j == J - 1),
                     )
+            if r % PAIR == PAIR - 1 and r // PAIR + AHEAD < PAIRS:
+                apply_mask(r // PAIR + AHEAD)
 
         abs_gamma = held.tile([P, 1], F32, name="abs_gamma")
         nc.scalar.activation(abs_gamma[:], gamma_all[:], FUNC.Abs)

@@ -61,7 +61,8 @@ def tile_binary_dense_kernel(tc, x, w, mask, gamma, offs, out):
             nc.scalar.activation(w_sign[r // PAIR][:, r % PAIR, :], w_raw[:, r, :], FUNC.Sign)
 
         def apply_mask(g):
-            nc.vector.tensor_tensor(
+            engine = nc.gpsimd if g > AHEAD and g % 2 == 1 else nc.vector
+            engine.tensor_tensor(
                 weights[g][:], w_sign[g][:], mask_bf16[:].unsqueeze(1).to_broadcast([P, PAIR, J * M]), ALU.mult
             )
 

@@ -1,5 +1,4 @@
 import concourse.mybir as mybir
-from concourse.masks import make_identity
 
 F32 = mybir.dt.float32
 BF16 = mybir.dt.bfloat16
@@ -12,15 +11,26 @@ C, S, M, R, T = 256, 512, 128, 16, 3
 CB = C // P
 J = S // P
 COLS = S // 16
+N3 = 2
+PATTERNS = R // N3
 PAIR = 2
 PAIRS = R // PAIR
-AHEAD = 2
+EARLY = 4
 
 FLOPS = 2 * C * R * S * M
 
 
 def every_jth(tile):
     return tile[:].rearrange("c (p j) -> c j p", j=J)
+
+
+def row_of(q):
+    code = N3 * (q % PATTERNS) + q // PATTERNS
+    return code ^ (code >> 1)
+
+
+def on_gpsimd(g):
+    return g > 1 and g % 2 == 1
 
 
 def tile_binary_dense_kernel(tc, x, w, mask, gamma, offs, out):
@@ -41,63 +51,75 @@ def tile_binary_dense_kernel(tc, x, w, mask, gamma, offs, out):
         nc.sync.dma_start(mask_f32[:], mask.rearrange("(p j) m -> p (j m)", j=J))
         w_by_partition = w.rearrange("r (p j) m -> p r (j m)", j=J)
         w_raw = held.tile([P, R, J * M], F32, name="w_raw")
-        for r in range(R):
-            nc.sync.dma_start(w_raw[:, r, :], w_by_partition[:, r, :])
+        for q in range(R):
+            nc.sync.dma_start(w_raw[:, q, :], w_by_partition[:, row_of(q), :])
         gamma_all = held.tile([P, 1], F32, name="gamma_all")
         nc.sync.dma_start(gamma_all[:], gamma.partition_broadcast(P))
 
-        eye = held.tile([P, P], F32, name="eye")
-        make_identity(nc, eye[:])
-        mask_bf16 = held.tile([P, J * M], BF16, name="mask_bf16")
-        nc.gpsimd.tensor_copy(mask_bf16[:], mask_f32[:])
         weighted_eye = [held.tile([P, P], BF16, name=f"weighted_eye{t}") for t in range(T)]
         for t in range(T):
-            nc.scalar.mul(weighted_eye[t][:], eye[:], float(2 ** (T - 1 - t)))
+            nc.gpsimd.memset(weighted_eye[t][:], 0.0)
+            nc.gpsimd.affine_select(
+                out=weighted_eye[t][:],
+                in_=weighted_eye[t][:],
+                compare_op=ALU.not_equal,
+                fill=float(2 ** (T - 1 - t)),
+                base=0,
+                pattern=[[-1, P]],
+                channel_multiplier=1,
+            )
+        mask_bf16 = held.tile([P, J * M], BF16, name="mask_bf16")
+        nc.gpsimd.tensor_copy(mask_bf16[:], mask_f32[:])
 
         w_sign = [held.tile([P, PAIR, J * M], BF16, name=f"w_sign{g}") for g in range(PAIRS)]
         weights = [held.tile([P, PAIR, J * M], BF16, name=f"weights{g}") for g in range(PAIRS)]
 
-        def take_sign(r):
-            nc.scalar.activation(w_sign[r // PAIR][:, r % PAIR, :], w_raw[:, r, :], FUNC.Sign)
+        def take_sign(q):
+            nc.scalar.activation(w_sign[q // PAIR][:, q % PAIR, :], w_raw[:, q, :], FUNC.Sign)
 
         def apply_mask(g):
-            engine = nc.gpsimd if g > AHEAD and g % 2 == 1 else nc.vector
+            engine = nc.gpsimd if on_gpsimd(g) else nc.vector
             engine.tensor_tensor(
                 weights[g][:], w_sign[g][:], mask_bf16[:].unsqueeze(1).to_broadcast([P, PAIR, J * M]), ALU.mult
             )
 
         sign_of = [[held.tile([P, S], BF16, name=f"sign_of{t}_{cb}") for cb in range(CB)] for t in range(T)]
+        signs_bank = [psum.tile([P, J, P], BF16, name=f"signs_bank{cb}") for cb in range(CB)]
         for t in range(T):
             for cb in range(CB):
                 looked_up = window[cb][:].indirect(offsets[:, t * COLS : (t + 1) * COLS])
                 nc.vector.tensor_tensor(chain[t + 1][cb][:], looked_up, chain[t][cb][:], ALU.mult)
                 nc.scalar.activation(sign_of[t][cb][:], chain[t][cb][:], FUNC.Sign)
-                if t > 0:
-                    take_sign((t - 1) * CB + cb)
-        for g in range(AHEAD):
-            apply_mask(g)
-
-        plain_eye = weighted_eye[T - 1]
-        magnitude_rows = [[held.tile([P, S], BF16, name=f"magnitude_rows{n3}_{cb}") for cb in range(CB)] for n3 in range(2)]
-        magnitude = [psum.tile([P, CB, J, P], BF16, name=f"magnitude{n3}") for n3 in range(2)]
-        signs_bank = [psum.tile([P, J, P], F32, name=f"signs_bank{cb}") for cb in range(CB)]
-        signs_turned = held.tile([P, CB, J, P], BF16, name="signs_turned")
-        matches = [held.tile([P, CB, J, P], BF16, name=f"matches{n}") for n in range(R // 2)]
-        for cb in range(CB):
-            for j in range(J):
-                for t in range(T):
+                for j in range(J):
                     nc.tensor.matmul(
                         signs_bank[cb][:, j, :],
                         lhsT=every_jth(sign_of[t][cb])[:, j, :],
                         rhs=weighted_eye[t][:],
-                        start=(t == 0),
-                        stop=(t == T - 1),
+                        start=(t == 0 and j == 0),
+                        stop=(t == T - 1 and j == J - 1),
                     )
+                if 0 <= (t - 1) * CB + cb < EARLY:
+                    take_sign((t - 1) * CB + cb)
+
+        plain_eye = weighted_eye[T - 1]
+        signs_turned = held.tile([P, CB, J, P], BF16, name="signs_turned")
+        magnitude_rows = [[held.tile([P, S], BF16, name=f"magnitude_rows{n3}_{cb}") for cb in range(CB)] for n3 in range(N3)]
+        magnitude = [psum.tile([P, CB, J, P], BF16, name=f"magnitude{n3}") for n3 in range(N3)]
         for cb in range(CB):
-            for n3 in range(2):
+            nc.vector.tensor_copy(signs_turned[:, cb], signs_bank[cb][:])
+        for n3 in range(N3):
+            for cb in range(CB):
                 nc.scalar.activation(magnitude_rows[n3][cb][:], chain[T][cb][:], FUNC.Relu, scale=1.0 - 2.0 * n3)
-            nc.scalar.copy(signs_turned[:, cb], signs_bank[cb][:])
-            for n3 in range(2):
+        for q in range(EARLY, 4 * PAIR):
+            take_sign(q)
+        for g in (5, 4, 7, 6):
+            for q in range(g * PAIR, (g + 1) * PAIR):
+                take_sign(q)
+            if on_gpsimd(g):
+                apply_mask(g)
+
+        def turn_magnitude(n3):
+            for cb in range(CB):
                 for j in range(J):
                     nc.tensor.matmul(
                         magnitude[n3][:, cb, j, :],
@@ -106,29 +128,35 @@ def tile_binary_dense_kernel(tc, x, w, mask, gamma, offs, out):
                         start=True,
                         stop=True,
                     )
-            for n in range(R // 2):
-                nc.vector.tensor_scalar(
-                    matches[n][:, cb], signs_turned[:, cb], float(R // 2 - 1 - 2 * n), None, ALU.is_equal
-                )
-        for r in range(AHEAD * PAIR, R):
-            take_sign(r)
 
+        matches = [held.tile([P, CB, J, P], BF16, name=f"matches{n}") for n in range(PATTERNS)]
         acc = [psum.tile([P, M], F32, name=f"acc{cb}") for cb in range(CB)]
-        for r in range(R):
-            code = r ^ (r >> 1) ^ (r >> 2) ^ (r >> 3)
-            f_row = held.tile([P, CB, J, P], BF16, name=f"f_row{r}")
-            nc.vector.tensor_tensor(f_row[:], magnitude[code & 1][:], matches[code >> 1][:], ALU.mult)
+        def make_matches(n):
+            nc.vector.tensor_scalar(matches[n][:], signs_turned[:], float(PATTERNS - 1 - 2 * n), None, ALU.is_equal)
+
+        apply_mask(0)
+        make_matches(0)
+        turn_magnitude(0)
+        apply_mask(3)
+        for q in range(R):
+            n3, n = q // PATTERNS, q % PATTERNS
+            if q % PAIR == 0 and q > 0 and not on_gpsimd(q // PAIR):
+                apply_mask(q // PAIR)
+            if n3 == 0 and n + 1 < PATTERNS:
+                make_matches(n + 1)
+            f_row = held.tile([P, CB, J, P], BF16, name=f"f_row{q}")
+            nc.vector.tensor_tensor(f_row[:], magnitude[n3][:], matches[n][:], ALU.mult)
             for j in range(J):
                 for cb in range(CB):
                     nc.tensor.matmul(
                         acc[cb][:],
                         lhsT=f_row[:, cb, j, :],
-                        rhs=weights[r // PAIR][:, r % PAIR, j * M : (j + 1) * M],
-                        start=(r == 0 and j == 0),
-                        stop=(r == R - 1 and j == J - 1),
+                        rhs=weights[q // PAIR][:, q % PAIR, j * M : (j + 1) * M],
+                        start=(q == 0 and j == 0),
+                        stop=(q == R - 1 and j == J - 1),
                     )
-            if r % PAIR == PAIR - 1 and r // PAIR + AHEAD < PAIRS:
-                apply_mask(r // PAIR + AHEAD)
+            if q == PAIR - 1:
+                turn_magnitude(1)
 
         abs_gamma = held.tile([P, 1], F32, name="abs_gamma")
         nc.scalar.activation(abs_gamma[:], gamma_all[:], FUNC.Abs)

@@ -77,10 +77,13 @@ def tile_binary_dense_kernel(tc, x, w, mask, gamma, offs, out):
         def take_sign(q):
             nc.scalar.activation(w_sign[q // PAIR][:, q % PAIR, :], w_raw[:, q, :], FUNC.Sign)
 
+        mask_psum = psum.tile([P, J * M], BF16, name="mask_psum")
+        nc.tensor.matmul(mask_psum[:], lhsT=weighted_eye[T - 1][:], rhs=mask_bf16[:], start=True, stop=True)
+
         def apply_mask(g):
-            engine = nc.gpsimd if on_gpsimd(g) else nc.vector
+            engine, mask_there = (nc.gpsimd, mask_bf16) if on_gpsimd(g) else (nc.vector, mask_psum)
             engine.tensor_tensor(
-                weights[g][:], w_sign[g][:], mask_bf16[:].unsqueeze(1).to_broadcast([P, PAIR, J * M]), ALU.mult
+                weights[g][:], w_sign[g][:], mask_there[:].unsqueeze(1).to_broadcast([P, PAIR, J * M]), ALU.mult
             )
 
         sign_of = [[held.tile([P, S], BF16, name=f"sign_of{t}_{cb}") for cb in range(CB)] for t in range(T)]
@@ -134,16 +137,15 @@ def tile_binary_dense_kernel(tc, x, w, mask, gamma, offs, out):
         def make_matches(n):
             nc.vector.tensor_scalar(matches[n][:], signs_turned[:], float(PATTERNS - 1 - 2 * n), None, ALU.is_equal)
 
+        for n in range(PATTERNS):
+            make_matches(n)
         apply_mask(0)
-        make_matches(0)
         turn_magnitude(0)
         apply_mask(3)
         for q in range(R):
             n3, n = q // PATTERNS, q % PATTERNS
             if q % PAIR == 0 and q > 0 and not on_gpsimd(q // PAIR):
                 apply_mask(q // PAIR)
-            if n3 == 0 and n + 1 < PATTERNS:
-                make_matches(n + 1)
             f_row = held.tile([P, CB, J, P], BF16, name=f"f_row{q}")
             nc.vector.tensor_tensor(f_row[:], magnitude[n3][:], matches[n][:], ALU.mult)
             for j in range(J):

@@ -69,7 +69,7 @@ def tile_binary_dense_kernel(tc, x, w, mask, gamma, offs, out):
                 channel_multiplier=1,
             )
         mask_bf16 = held.tile([P, J * M], BF16, name="mask_bf16")
-        nc.gpsimd.tensor_copy(mask_bf16[:], mask_f32[:])
+        nc.scalar.copy(mask_bf16[:], mask_f32[:])
 
         w_sign = [held.tile([P, PAIR, J * M], BF16, name=f"w_sign{g}") for g in range(PAIRS)]
         weights = [held.tile([P, PAIR, J * M], BF16, name=f"weights{g}") for g in range(PAIRS)]

@@ -164,5 +164,5 @@ def tile_binary_dense_kernel(tc, x, w, mask, gamma, offs, out):
         nc.scalar.activation(abs_gamma[:], gamma_all[:], FUNC.Abs)
         for cb in range(CB):
             scaled = held.tile([P, M], F32, name=f"scaled{cb}")
-            nc.vector.tensor_scalar_mul(scaled[:], acc[cb][:], abs_gamma[:, 0:1])
+            nc.scalar.activation(scaled[:], acc[cb][:], FUNC.Copy, scale=abs_gamma[:, 0:1])
             nc.sync.dma_start(out[cb * P : (cb + 1) * P, :], scaled[:])

@@ -148,8 +148,8 @@ def tile_binary_dense_kernel(tc, x, w, mask, gamma, offs, out):
                 apply_mask(q // PAIR)
             f_row = held.tile([P, CB, J, P], BF16, name=f"f_row{q}")
             nc.vector.tensor_tensor(f_row[:], magnitude[n3][:], matches[n][:], ALU.mult)
-            for j in range(J):
-                for cb in range(CB):
+            for cb in range(CB):
+                for j in range(J):
                     nc.tensor.matmul(
                         acc[cb][:],
                         lhsT=f_row[:, cb, j, :],

@@ -30,7 +30,7 @@ def row_of(q):
 
 
 def on_gpsimd(g):
-    return g > 1 and g % 2 == 1
+    return g in (2, 4, 6, 7)
 
 
 def tile_binary_dense_kernel(tc, x, w, mask, gamma, offs, out):
@@ -113,9 +113,7 @@ def tile_binary_dense_kernel(tc, x, w, mask, gamma, offs, out):
         for n3 in range(N3):
             for cb in range(CB):
                 nc.scalar.activation(magnitude_rows[n3][cb][:], chain[T][cb][:], FUNC.Relu, scale=1.0 - 2.0 * n3)
-        for q in range(EARLY, 4 * PAIR):
-            take_sign(q)
-        for g in (5, 4, 7, 6):
+        for g in range(EARLY // PAIR, PAIRS):
             for q in range(g * PAIR, (g + 1) * PAIR):
                 take_sign(q)
             if on_gpsimd(g):
@@ -141,7 +139,6 @@ def tile_binary_dense_kernel(tc, x, w, mask, gamma, offs, out):
             make_matches(n)
         apply_mask(0)
         turn_magnitude(0)
-        apply_mask(3)
         for q in range(R):
             n3, n = q // PATTERNS, q % PATTERNS
             if q % PAIR == 0 and q > 0 and not on_gpsimd(q // PAIR):

@@ -162,4 +162,4 @@ def tile_binary_dense_kernel(tc, x, w, mask, gamma, offs, out):
         for cb in range(CB):
             scaled = held.tile([P, M], F32, name=f"scaled{cb}")
             nc.scalar.activation(scaled[:], acc[cb][:], FUNC.Copy, scale=abs_gamma[:, 0:1])
-            nc.sync.dma_start(out[cb * P : (cb + 1) * P, :], scaled[:])
+            nc.scalar.dma_start(out[cb * P : (cb + 1) * P, :], scaled[:])

@@ -16,6 +16,7 @@ PATTERNS = R // N3
 PAIR = 2
 PAIRS = R // PAIR
 EARLY = 4
+FIRST_CUT = 128
 
 FLOPS = 2 * C * R * S * M
 
@@ -42,11 +43,15 @@ def tile_binary_dense_kernel(tc, x, w, mask, gamma, offs, out):
         offsets = held.tile([P, T * COLS], U16, name="offsets")
         nc.sync.dma_start(offsets[:], offs)
         window = [held.tile([P, S], F32, name=f"window{cb}") for cb in range(CB)]
-        chain = [[held.tile([P, S], F32, name=f"chain{t}_{cb}") for cb in range(CB)] for t in range(T + 1)]
-        for cb in range(CB):
-            samples = x[cb * P : (cb + 1) * P, :]
-            nc.sync.dma_start(window[cb][:], samples)
-            nc.sync.dma_start(chain[0][cb][:], samples)
+        chain = [[window[0], held.tile([P, S], F32, name="chain0_1")]]
+        chain += [[held.tile([P, S], F32, name=f"chain{t}_{cb}") for cb in range(CB)] for t in range(1, T + 1)]
+        first_pieces = ((0, FIRST_CUT), (FIRST_CUT, S))
+        first_factor = [held.tile([P, b - a], F32, name=f"first_factor{a}") for a, b in first_pieces]
+        nc.sync.dma_start(window[0][:], x[0:P, :])
+        for (a, b), factor in zip(first_pieces, first_factor):
+            nc.sync.dma_start(factor[:], x[0:P, a:b])
+        nc.sync.dma_start(window[1][:], x[P : 2 * P, :])
+        nc.sync.dma_start(chain[0][1][:], x[P : 2 * P, :])
         mask_f32 = held.tile([P, J * M], F32, name="mask_f32")
         nc.sync.dma_start(mask_f32[:], mask.rearrange("(p j) m -> p (j m)", j=J))
         w_by_partition = w.rearrange("r (p j) m -> p r (j m)", j=J)
@@ -90,8 +95,13 @@ def tile_binary_dense_kernel(tc, x, w, mask, gamma, offs, out):
         signs_bank = [psum.tile([P, J, P], BF16, name=f"signs_bank{cb}") for cb in range(CB)]
         for t in range(T):
             for cb in range(CB):
-                looked_up = window[cb][:].indirect(offsets[:, t * COLS : (t + 1) * COLS])
-                nc.vector.tensor_tensor(chain[t + 1][cb][:], looked_up, chain[t][cb][:], ALU.mult)
+                if (t, cb) == (0, 0):
+                    for (a, b), factor in zip(first_pieces, first_factor):
+                        looked_up = window[0][:].indirect(offsets[:, a // 16 : b // 16])
+                        nc.vector.tensor_tensor(chain[1][0][:, a:b], looked_up, factor[:], ALU.mult)
+                else:
+                    looked_up = window[cb][:].indirect(offsets[:, t * COLS : (t + 1) * COLS])
+                    nc.vector.tensor_tensor(chain[t + 1][cb][:], looked_up, chain[t][cb][:], ALU.mult)
                 nc.scalar.activation(sign_of[t][cb][:], chain[t][cb][:], FUNC.Sign)
                 for j in range(J):
                     nc.tensor.matmul(

import concourse.mybir as mybir

F32 = mybir.dt.float32
BF16 = mybir.dt.bfloat16
U16 = mybir.dt.uint16
ALU = mybir.AluOpType
FUNC = mybir.ActivationFunctionType

P = 128
C, S, M, R, T = 256, 512, 128, 16, 3
CB = C // P
J = S // P
COLS = S // 16
N3 = 2
PATTERNS = R // N3
PAIR = 2
PAIRS = R // PAIR
EARLY = 4
FIRST_CUT = 128

FLOPS = 2 * C * R * S * M


def every_jth(tile):
    return tile[:].rearrange("c (p j) -> c j p", j=J)


def row_of(q):
    code = N3 * (q % PATTERNS) + q // PATTERNS
    return code ^ (code >> 1)


def on_gpsimd(g):
    return g in (2, 4, 6, 7)


def tile_binary_dense_kernel(tc, x, w, mask, gamma, offs, out):
    nc = tc.nc
    with (
        tc.tile_pool(name="held", bufs=1) as held,
        tc.psum_pool(name="psum", bufs=1) as psum,
    ):
        offsets = held.tile([P, T * COLS], U16, name="offsets")
        nc.sync.dma_start(offsets[:], offs)
        window = [held.tile([P, S], F32, name=f"window{cb}") for cb in range(CB)]
        chain = [[window[0], held.tile([P, S], F32, name="chain0_1")]]
        chain += [[held.tile([P, S], F32, name=f"chain{t}_{cb}") for cb in range(CB)] for t in range(1, T + 1)]
        first_pieces = ((0, FIRST_CUT), (FIRST_CUT, S))
        first_factor = [held.tile([P, b - a], F32, name=f"first_factor{a}") for a, b in first_pieces]
        nc.sync.dma_start(window[0][:], x[0:P, :])
        for (a, b), factor in zip(first_pieces, first_factor):
            nc.sync.dma_start(factor[:], x[0:P, a:b])
        nc.sync.dma_start(window[1][:], x[P : 2 * P, :])
        nc.sync.dma_start(chain[0][1][:], x[P : 2 * P, :])
        mask_f32 = held.tile([P, J * M], F32, name="mask_f32")
        nc.sync.dma_start(mask_f32[:], mask.rearrange("(p j) m -> p (j m)", j=J))
        w_by_partition = w.rearrange("r (p j) m -> p r (j m)", j=J)
        w_raw = held.tile([P, R, J * M], F32, name="w_raw")
        for q in range(R):
            nc.sync.dma_start(w_raw[:, q, :], w_by_partition[:, row_of(q), :])
        gamma_all = held.tile([P, 1], F32, name="gamma_all")
        nc.sync.dma_start(gamma_all[:], gamma.partition_broadcast(P))

        weighted_eye = [held.tile([P, P], BF16, name=f"weighted_eye{t}") for t in range(T)]
        for t in range(T):
            nc.gpsimd.memset(weighted_eye[t][:], 0.0)
            nc.gpsimd.affine_select(
                out=weighted_eye[t][:],
                in_=weighted_eye[t][:],
                compare_op=ALU.not_equal,
                fill=float(2 ** (T - 1 - t)),
                base=0,
                pattern=[[-1, P]],
                channel_multiplier=1,
            )
        mask_bf16 = held.tile([P, J * M], BF16, name="mask_bf16")
        nc.scalar.copy(mask_bf16[:], mask_f32[:])

        w_sign = [held.tile([P, PAIR, J * M], BF16, name=f"w_sign{g}") for g in range(PAIRS)]
        weights = [held.tile([P, PAIR, J * M], BF16, name=f"weights{g}") for g in range(PAIRS)]

        def take_sign(q):
            nc.scalar.activation(w_sign[q // PAIR][:, q % PAIR, :], w_raw[:, q, :], FUNC.Sign)

        mask_psum = psum.tile([P, J * M], BF16, name="mask_psum")
        nc.tensor.matmul(mask_psum[:], lhsT=weighted_eye[T - 1][:], rhs=mask_bf16[:], start=True, stop=True)

        def apply_mask(g):
            engine, mask_there = (nc.gpsimd, mask_bf16) if on_gpsimd(g) else (nc.vector, mask_psum)
            engine.tensor_tensor(
                weights[g][:], w_sign[g][:], mask_there[:].unsqueeze(1).to_broadcast([P, PAIR, J * M]), ALU.mult
            )

        sign_of = [[held.tile([P, S], BF16, name=f"sign_of{t}_{cb}") for cb in range(CB)] for t in range(T)]
        signs_bank = [psum.tile([P, J, P], BF16, name=f"signs_bank{cb}") for cb in range(CB)]
        for t in range(T):
            for cb in range(CB):
                if (t, cb) == (0, 0):
                    for (a, b), factor in zip(first_pieces, first_factor):
                        looked_up = window[0][:].indirect(offsets[:, a // 16 : b // 16])
                        nc.vector.tensor_tensor(chain[1][0][:, a:b], looked_up, factor[:], ALU.mult)
                else:
                    looked_up = window[cb][:].indirect(offsets[:, t * COLS : (t + 1) * COLS])
                    nc.vector.tensor_tensor(chain[t + 1][cb][:], looked_up, chain[t][cb][:], ALU.mult)
                nc.scalar.activation(sign_of[t][cb][:], chain[t][cb][:], FUNC.Sign)
                for j in range(J):
                    nc.tensor.matmul(
                        signs_bank[cb][:, j, :],
                        lhsT=every_jth(sign_of[t][cb])[:, j, :],
                        rhs=weighted_eye[t][:],
                        start=(t == 0 and j == 0),
                        stop=(t == T - 1 and j == J - 1),
                    )
                if 0 <= (t - 1) * CB + cb < EARLY:
                    take_sign((t - 1) * CB + cb)

        plain_eye = weighted_eye[T - 1]
        signs_turned = held.tile([P, CB, J, P], BF16, name="signs_turned")
        magnitude_rows = [[held.tile([P, S], BF16, name=f"magnitude_rows{n3}_{cb}") for cb in range(CB)] for n3 in range(N3)]
        magnitude = [psum.tile([P, CB, J, P], BF16, name=f"magnitude{n3}") for n3 in range(N3)]
        for cb in range(CB):
            nc.vector.tensor_copy(signs_turned[:, cb], signs_bank[cb][:])
        for n3 in range(N3):
            for cb in range(CB):
                nc.scalar.activation(magnitude_rows[n3][cb][:], chain[T][cb][:], FUNC.Relu, scale=1.0 - 2.0 * n3)
        for g in range(EARLY // PAIR, PAIRS):
            for q in range(g * PAIR, (g + 1) * PAIR):
                take_sign(q)
            if on_gpsimd(g):
                apply_mask(g)

        def turn_magnitude(n3):
            for cb in range(CB):
                for j in range(J):
                    nc.tensor.matmul(
                        magnitude[n3][:, cb, j, :],
                        lhsT=every_jth(magnitude_rows[n3][cb])[:, j, :],
                        rhs=plain_eye[:],
                        start=True,
                        stop=True,
                    )

        matches = [held.tile([P, CB, J, P], BF16, name=f"matches{n}") for n in range(PATTERNS)]
        acc = [psum.tile([P, M], F32, name=f"acc{cb}") for cb in range(CB)]
        def make_matches(n):
            nc.vector.tensor_scalar(matches[n][:], signs_turned[:], float(PATTERNS - 1 - 2 * n), None, ALU.is_equal)

        for n in range(PATTERNS):
            make_matches(n)
        apply_mask(0)
        turn_magnitude(0)
        for q in range(R):
            n3, n = q // PATTERNS, q % PATTERNS
            if q % PAIR == 0 and q > 0 and not on_gpsimd(q // PAIR):
                apply_mask(q // PAIR)
            f_row = held.tile([P, CB, J, P], BF16, name=f"f_row{q}")
            nc.vector.tensor_tensor(f_row[:], magnitude[n3][:], matches[n][:], ALU.mult)
            for cb in range(CB):
                for j in range(J):
                    nc.tensor.matmul(
                        acc[cb][:],
                        lhsT=f_row[:, cb, j, :],
                        rhs=weights[q // PAIR][:, q % PAIR, j * M : (j + 1) * M],
                        start=(q == 0 and j == 0),
                        stop=(q == R - 1 and j == J - 1),
                    )
            if q == PAIR - 1:
                turn_magnitude(1)

        abs_gamma = held.tile([P, 1], F32, name="abs_gamma")
        nc.scalar.activation(abs_gamma[:], gamma_all[:], FUNC.Abs)
        for cb in range(CB):
            scaled = held.tile([P, M], F32, name=f"scaled{cb}")
            nc.scalar.activation(scaled[:], acc[cb][:], FUNC.Copy, scale=abs_gamma[:, 0:1])
            nc.scalar.dma_start(out[cb * P : (cb + 1) * P, :], scaled[:])
